import numpy as np
import ml_dtypes


def mxq(x, axis, fmt="e4m3"):
    dtype, down = {"e4m3": (ml_dtypes.float8_e4m3fn, 7), "e5m2": (ml_dtypes.float8_e5m2, 14)}[fmt]
    v = np.moveaxis(np.asarray(x, np.float32).astype(ml_dtypes.bfloat16).astype(np.float64), axis, -1)
    blocks = v.reshape(v.shape[:-1] + (-1, 32))
    amax = np.abs(blocks).max(-1, keepdims=True)
    byte = np.maximum(np.where(amax > 0, np.frexp(amax)[1] - 1 + 127, 0) - down, 1)
    scale = np.exp2(byte - 127.0)
    codes = (blocks / scale).astype(np.float32).astype(dtype).astype(np.float64)
    return np.moveaxis((codes * scale).reshape(v.shape), -1, axis)


WIDE = False


def mx_kscale(k):
    if not WIDE:
        return np.ones(k)
    levels = np.array([10, -10, 5, -5, 0])
    a = np.random.permutation(np.resize(levels, k // 512 * 4)).reshape(k // 512, 4)
    idx = np.arange(k)
    return np.exp2(a[idx // 512, idx % 128 // 32])


BF16 = ml_dtypes.bfloat16


def bf(x):
    return np.asarray(x, np.float32).astype(BF16)


def f64(x):
    return np.asarray(x).astype(np.float64)


E2M1 = np.array([0.0, 0.5, 1.0, 1.5, 2.0, 3.0, 4.0, 6.0, -0.0, -0.5, -1.0, -1.5, -2.0, -3.0, -4.0, -6.0])


def pack_weight(w, fmt):
    k, n = w.shape
    w = f64(bf(w)).reshape(k // 32, 32, n)
    amax = np.abs(w).max(1)
    if fmt == "e4m3":
        byte = np.frexp(amax)[1] - 1 + 127 - 7
    else:
        mant, ex = np.frexp(amax / 6.0)
        byte = np.where(mant > 0.5, ex, ex - 1) + 127
    byte = np.clip(np.where(amax > 0, byte, 1), 1, 254)
    scaled = (w * np.exp2(127.0 - byte)[:, None, :]).reshape(k, n).astype(np.float32)
    by_word = np.ascontiguousarray(scaled.reshape(k // 512, 128, 4, n).transpose(0, 1, 3, 2))
    if fmt == "e4m3":
        words = by_word.astype(ml_dtypes.float8_e4m3fn).view(np.uint8)
    else:
        c = by_word.astype(ml_dtypes.float4_e2m1fn).view(np.uint8) & 0xF
        words = c[..., 0::2] | (c[..., 1::2] << 4)
    return np.ascontiguousarray(words), np.ascontiguousarray(byte.astype(np.uint8).reshape(k // 512, 16, n))


def unpack_weight(words, scales, fmt):
    g, p, n, _ = words.shape
    if fmt == "e4m3":
        vals = np.ascontiguousarray(words).view(ml_dtypes.float8_e4m3fn).astype(np.float64)
    else:
        nib = np.empty((g, p, n, 4), np.uint8)
        nib[..., 0::2] = words & 0xF
        nib[..., 1::2] = words >> 4
        vals = E2M1[nib]
    vals = vals * np.repeat(np.exp2(scales.astype(np.float64) - 127.0), 8, axis=1)[..., None]
    return vals.transpose(0, 1, 3, 2).reshape(g * 512, n)

def pack4(w):
    words, scales = pack_weight(w, "e2m1")
    return words.reshape(words.shape[0], 128, -1), scales


def unpack4(words, scales):
    return unpack_weight(words.reshape(words.shape[0], 128, -1, 2), scales, "e2m1")


B, N, D1, D2, F1, F2, F3, F4 = 8192, 1, 256, 256, 512, 64, 32, 16
K = D1 + D2
EPS = 1e-5
SLOPE = 0.2


def setup_inputs():
    s = mx_kscale(K)
    g = np.sqrt(EPS)
    input1 = bf(np.random.standard_normal((B, N, D1)) * s[:D1])
    input2 = bf(np.random.standard_normal((B, N, D2)) * s[D1:])
    w1 = np.random.standard_normal((F1, K)) * 5.0 * g / np.sqrt(K) / s[None, :]
    words, scales = pack4(np.ascontiguousarray(w1.T))
    b1 = bf(np.random.standard_normal(F1) * 2.5 * g)
    return {"input1": input1,
            "input2": input2,
            "W1_words": words,
            "W1_scales": scales,
            "b1": b1}


def reference(input1, input2, W1_words, W1_scales, b1):
    x = np.concatenate([f64(input1), f64(input2)], axis=2)
    h = (mxq(x, 2, "e4m3") @ unpack4(W1_words, W1_scales)) + f64(b1)
    m = h.mean(axis=-1, keepdims=True)
    v = np.square(h - m).mean(axis=-1, keepdims=True)
    hn = (h - m) * (1.0 / np.sqrt(v + EPS))
    return np.where(hn >= 0, hn, SLOPE * hn)

@@ -1,0 +1,204 @@
+from contextlib import ExitStack
+
+import concourse.mybir as mybir
+from concourse.masks import make_identity
+
+F32 = mybir.dt.float32
+BF16 = mybir.dt.bfloat16
+I32 = mybir.dt.int32
+U32 = mybir.dt.uint32
+U8 = mybir.dt.uint8
+FP8X4 = mybir.dt.float8_e4m3fn_x4
+FP4X4 = mybir.dt.float4_e2m1fn_x4
+ACT = mybir.ActivationFunctionType
+ALU = mybir.AluOpType
+
+P = 128
+ROWS = 8192
+D_IN = 256
+K = 2 * D_IN
+WORDS = K // 2
+FEATURES = 512
+EPS = 1e-5
+SLOPE = 0.2
+
+TILES = 4
+PAIRS = TILES // 2
+N_GROUPS = ROWS // (TILES * P)
+
+FLOPS = 2 * ROWS * K * FEATURES
+
+
+def tile_fcd_pa_t_kernel(tc, input1, input2, W1_words, W1_scales, b1, out):
+    nc = tc.nc
+
+    x1_groups = input1.rearrange("(g p j) o d -> g p j (o d)", p=P, j=TILES)
+    x2_groups = input2.rearrange("(g p j) o d -> g p j (o d)", p=P, j=TILES)
+    out_groups = out.rearrange("(g p j) o f -> g p j (o f)", p=P, j=TILES)
+
+    with ExitStack() as ctx:
+        const = ctx.enter_context(tc.tile_pool(name="const", bufs=1))
+        x_pool = ctx.enter_context(tc.tile_pool(name="x", bufs=1))
+        quant = ctx.enter_context(tc.tile_pool(name="quant", bufs=2))
+        h_pool = ctx.enter_context(tc.tile_pool(name="h", bufs=3))
+        y_pool = ctx.enter_context(tc.tile_pool(name="y", bufs=6))
+        stats = ctx.enter_context(tc.tile_pool(name="stats", bufs=3))
+        xt_psum = ctx.enter_context(tc.psum_pool(name="xt_psum", bufs=2 * PAIRS))
+        h_psum = ctx.enter_context(tc.psum_pool(name="h_psum", bufs=TILES))
+
+        ident = const.tile([P, P], F32)
+        make_identity(nc, ident[:])
+        eps = const.tile([P, 1], F32)
+        nc.vector.memset(eps[:], EPS)
+        warm = const.tile([P, 1], F32)
+        nc.scalar.activation(out=warm[:], in_=eps[:], func=ACT.Sqrt)
+        squares = const.tile([P, FEATURES], F32)
+
+        w_words = const.tile([P, 2 * FEATURES], U8, align_bytes=64)
+        w_scales = const.tile([P, FEATURES], U8, align_bytes=64)
+        nc.vector.memset(w_scales[:].bitcast(I32), 0)
+        bias = const.tile([P, FEATURES], BF16)
+
+        x_tiles = []
+        for g in range(N_GROUPS):
+            x_sb = x_pool.tile([P, TILES, K], BF16, name="x%d" % g)
+            nc.sync.dma_start(out=x_sb[:, :, 0:D_IN], in_=x1_groups[g])
+            nc.sync.dma_start(out=x_sb[:, :, D_IN:K], in_=x2_groups[g])
+            x_tiles.append(x_sb)
+            if g == 0:
+                nc.sync.dma_start(out=w_words[:].bitcast(I32), in_=W1_words[0].bitcast(I32))
+                for quadrant in range(4):
+                    nc.sync.dma_start(
+                        out=w_scales[32 * quadrant : 32 * quadrant + 4, :].bitcast(I32),
+                        in_=W1_scales[0, 4 * quadrant : 4 * quadrant + 4, :].bitcast(I32),
+                    )
+                nc.sync.dma_start(out=bias[:], in_=b1.partition_broadcast(P))
+
+        xt_banks = {}
+        grouped_of = {}
+        product_of = {}
+        h_of = {}
+        negmean_of = {}
+        std_of = {}
+        rstd_of = {}
+        shift_of = {}
+        y_of = {}
+
+        def transpose(g):
+            x_words = x_tiles[g][:].bitcast(F32)
+            xt_banks[g] = []
+            for pair in range(PAIRS):
+                xt = xt_psum.tile([P, 2, 2, P], F32)
+                for j in range(2):
+                    for u in range(2):
+                        nc.tensor.transpose(
+                            xt[:, j, u, :], x_words[:, 2 * pair + j, u:WORDS:2], ident[:]
+                        )
+                xt_banks[g].append(xt)
+
+        def evacuate(g):
+            grouped = quant.tile([P, TILES * K], BF16, align_bytes=64)
+            words = grouped[:].bitcast(F32).rearrange("p (j r u) -> p j r u", j=TILES, u=2)
+            for pair in range(PAIRS):
+                nc.scalar.copy(
+                    out=words[:, 2 * pair : 2 * pair + 2],
+                    in_=xt_banks[g][pair][:].rearrange("p j u r -> p j r u"),
+                )
+            grouped_of[g] = grouped
+
+        def quantise_and_multiply(g):
+            codes = quant.tile([P, TILES * P], U32, align_bytes=64)
+            scales = quant.tile([P, TILES * P], U8, align_bytes=64)
+            nc.vector.quantize_mx(
+                out=codes[:].bitcast(FP8X4), scales=scales[:], in_=grouped_of[g][:]
+            )
+            product_of[g] = []
+            for j in range(TILES):
+                rows = slice(j * P, (j + 1) * P)
+                product = h_psum.tile([P, FEATURES], F32)
+                nc.tensor.matmul_mx(
+                    out=product[:],
+                    lhsT=codes[:, rows].bitcast(FP8X4),
+                    lhsT_scale=scales[:, rows],
+                    rhs=w_words[:].bitcast(FP4X4),
+                    rhs_scale=w_scales[:],
+                    start=True,
+                    stop=True,
+                )
+                product_of[g].append(product)
+
+        def add_bias(g):
+            h = h_pool.tile([P, TILES, FEATURES], F32)
+            row_sum = stats.tile([P, TILES], F32)
+            for j in range(TILES):
+                nc.vector.scalar_tensor_tensor(
+                    out=h[:, j, :],
+                    in0=product_of[g][j][:],
+                    scalar=1.0,
+                    in1=bias[:],
+                    op0=ALU.mult,
+                    op1=ALU.add,
+                    accum_out=row_sum[:, j : j + 1],
+                )
+            negmean = stats.tile([P, TILES], F32)
+            nc.vector.tensor_scalar_mul(out=negmean[:], in0=row_sum[:], scalar1=-1.0 / FEATURES)
+            h_of[g] = h
+            negmean_of[g] = negmean
+
+        def variance(g):
+            sum_sq = stats.tile([P, TILES], F32)
+            for j in range(TILES):
+                nc.scalar.activation(
+                    out=squares[:],
+                    in_=h_of[g][:, j, :],
+                    func=ACT.Square,
+                    bias=negmean_of[g][:, j : j + 1],
+                    scale=1.0,
+                    accum_out=sum_sq[:, j : j + 1],
+                )
+            std = stats.tile([P, TILES], F32)
+            nc.scalar.activation(
+                out=std[:], in_=sum_sq[:], func=ACT.Sqrt, bias=eps[:], scale=1.0 / FEATURES
+            )
+            std_of[g] = std
+
+        def scale_and_shift(g):
+            rstd = stats.tile([P, TILES], F32)
+            nc.vector.reciprocal(out=rstd[:], in_=std_of[g][:])
+            shift = stats.tile([P, TILES], F32)
+            nc.vector.tensor_mul(out=shift[:], in0=negmean_of[g][:], in1=rstd[:])
+            rstd_of[g] = rstd
+            shift_of[g] = shift
+
+        def normalise(g):
+            y = y_pool.tile([P, TILES, FEATURES], F32)
+            for j in range(TILES):
+                nc.scalar.activation(
+                    out=y[:, j, :],
+                    in_=h_of[g][:, j, :],
+                    func=ACT.Identity,
+                    bias=shift_of[g][:, j : j + 1],
+                    scale=rstd_of[g][:, j : j + 1],
+                )
+            y_of[g] = y
+
+        def leaky_relu_and_store(g):
+            flat = y_of[g][:].rearrange("p j f -> p (j f)")
+            nc.vector.scalar_tensor_tensor(
+                out=flat, in0=flat, scalar=SLOPE, in1=flat, op0=ALU.mult, op1=ALU.max
+            )
+            nc.sync.dma_start(out=out_groups[g], in_=y_of[g][:])
+
+        def run(stage, g):
+            if 0 <= g < N_GROUPS:
+                stage(g)
+
+        for step in range(-2, N_GROUPS + 1):
+            run(scale_and_shift, step - 1)
+            run(evacuate, step + 1)
+            run(transpose, step + 2)
+            run(add_bias, step)
+            run(normalise, step - 1)
+            run(quantise_and_multiply, step + 1)
+            run(variance, step)
+            run(leaky_relu_and_store, step - 1)

@@ -24,6 +24,7 @@ SLOPE = 0.2
 
 TILES = 4
 PAIRS = TILES // 2
+SCALAR_TILES = 3
 N_GROUPS = ROWS // (TILES * P)
 
 FLOPS = 2 * ROWS * K * FEATURES
@@ -78,7 +79,7 @@ def tile_fcd_pa_t_kernel(tc, input1, input2, W1_words, W1_scales, b1, out):
         grouped_of = {}
         product_of = {}
         h_of = {}
-        negmean_of = {}
+        row_sum_of = {}
         std_of = {}
         rstd_of = {}
         shift_of = {}
@@ -140,10 +141,8 @@ def tile_fcd_pa_t_kernel(tc, input1, input2, W1_words, W1_scales, b1, out):
                     op1=ALU.add,
                     accum_out=row_sum[:, j : j + 1],
                 )
-            negmean = stats.tile([P, TILES], F32)
-            nc.vector.tensor_scalar_mul(out=negmean[:], in0=row_sum[:], scalar1=-1.0 / FEATURES)
             h_of[g] = h
-            negmean_of[g] = negmean
+            row_sum_of[g] = row_sum
 
         def variance(g):
             sum_sq = stats.tile([P, TILES], F32)
@@ -152,13 +151,13 @@ def tile_fcd_pa_t_kernel(tc, input1, input2, W1_words, W1_scales, b1, out):
                     out=squares[:],
                     in_=h_of[g][:, j, :],
                     func=ACT.Square,
-                    bias=negmean_of[g][:, j : j + 1],
-                    scale=1.0,
+                    bias=row_sum_of[g][:, j : j + 1],
+                    scale=-float(FEATURES),
                     accum_out=sum_sq[:, j : j + 1],
                 )
             std = stats.tile([P, TILES], F32)
             nc.scalar.activation(
-                out=std[:], in_=sum_sq[:], func=ACT.Sqrt, bias=eps[:], scale=1.0 / FEATURES
+                out=std[:], in_=sum_sq[:], func=ACT.Sqrt, bias=eps[:], scale=1.0 / FEATURES**3
             )
             std_of[g] = std
 
@@ -166,13 +165,29 @@ def tile_fcd_pa_t_kernel(tc, input1, input2, W1_words, W1_scales, b1, out):
             rstd = stats.tile([P, TILES], F32)
             nc.vector.reciprocal(out=rstd[:], in_=std_of[g][:])
             shift = stats.tile([P, TILES], F32)
-            nc.vector.tensor_mul(out=shift[:], in0=negmean_of[g][:], in1=rstd[:])
+            nc.vector.scalar_tensor_tensor(
+                out=shift[:],
+                in0=row_sum_of[g][:],
+                scalar=-1.0 / FEATURES,
+                in1=rstd[:],
+                op0=ALU.mult,
+                op1=ALU.mult,
+            )
             rstd_of[g] = rstd
             shift_of[g] = shift
 
         def normalise(g):
             y = y_pool.tile([P, TILES, FEATURES], F32)
-            for j in range(TILES):
+            for j in range(SCALAR_TILES, TILES):
+                nc.vector.tensor_scalar(
+                    out=y[:, j, :],
+                    in0=h_of[g][:, j, :],
+                    scalar1=rstd_of[g][:, j : j + 1],
+                    scalar2=shift_of[g][:, j : j + 1],
+                    op0=ALU.mult,
+                    op1=ALU.add,
+                )
+            for j in range(SCALAR_TILES):
                 nc.scalar.activation(
                     out=y[:, j, :],
                     in_=h_of[g][:, j, :],
@@ -193,12 +208,13 @@ def tile_fcd_pa_t_kernel(tc, input1, input2, W1_words, W1_scales, b1, out):
             if 0 <= g < N_GROUPS:
                 stage(g)
 
-        for step in range(-2, N_GROUPS + 1):
-            run(scale_and_shift, step - 1)
-            run(evacuate, step + 1)
-            run(transpose, step + 2)
-            run(add_bias, step)
-            run(normalise, step - 1)
-            run(quantise_and_multiply, step + 1)
-            run(variance, step)
-            run(leaky_relu_and_store, step - 1)
+        with tc.manual_schedule():
+            for step in range(-2, N_GROUPS + 2):
+                run(scale_and_shift, step - 1)
+                run(evacuate, step + 1)
+                run(transpose, step + 2)
+                run(add_bias, step)
+                run(quantise_and_multiply, step + 1)
+                run(variance, step)
+                run(normalise, step - 1)
+                run(leaky_relu_and_store, step - 2)

@@ -49,10 +49,8 @@ def tile_fcd_pa_t_kernel(tc, input1, input2, W1_words, W1_scales, b1, out):
 
         ident = const.tile([P, P], F32)
         make_identity(nc, ident[:])
-        eps = const.tile([P, 1], F32)
-        nc.vector.memset(eps[:], EPS)
-        warm = const.tile([P, 1], F32)
-        nc.scalar.activation(out=warm[:], in_=eps[:], func=ACT.Sqrt)
+        minus_half = const.tile([P, TILES], F32)
+        nc.vector.memset(minus_half[:], -0.5)
         squares = const.tile([P, FEATURES], F32)
 
         w_words = const.tile([P, 2 * FEATURES], U8, align_bytes=64)
@@ -80,7 +78,7 @@ def tile_fcd_pa_t_kernel(tc, input1, input2, W1_words, W1_scales, b1, out):
         product_of = {}
         h_of = {}
         row_sum_of = {}
-        std_of = {}
+        sum_sq_of = {}
         rstd_of = {}
         shift_of = {}
         y_of = {}
@@ -155,31 +153,38 @@ def tile_fcd_pa_t_kernel(tc, input1, input2, W1_words, W1_scales, b1, out):
                     scale=-float(FEATURES),
                     accum_out=sum_sq[:, j : j + 1],
                 )
-            std = stats.tile([P, TILES], F32)
-            nc.scalar.activation(
-                out=std[:], in_=sum_sq[:], func=ACT.Sqrt, bias=eps[:], scale=1.0 / FEATURES**3
-            )
-            std_of[g] = std
+            sum_sq_of[g] = sum_sq
 
         def scale_and_shift(g):
-            rstd = stats.tile([P, TILES], F32)
-            nc.vector.reciprocal(out=rstd[:], in_=std_of[g][:])
-            shift = stats.tile([P, TILES], F32)
-            nc.vector.scalar_tensor_tensor(
-                out=shift[:],
+            negmean = stats.tile([P, TILES], F32)
+            nc.gpsimd.tensor_scalar(
+                out=negmean[:],
                 in0=row_sum_of[g][:],
-                scalar=-1.0 / FEATURES,
-                in1=rstd[:],
+                scalar1=-1.0 / FEATURES,
+                scalar2=0.0,
                 op0=ALU.mult,
-                op1=ALU.mult,
+                op1=ALU.add,
             )
+            var_eps = stats.tile([P, TILES], F32)
+            nc.gpsimd.tensor_scalar(
+                out=var_eps[:],
+                in0=sum_sq_of[g][:],
+                scalar1=1.0 / FEATURES**3,
+                scalar2=EPS,
+                op0=ALU.mult,
+                op1=ALU.add,
+            )
+            rstd = stats.tile([P, TILES], F32)
+            nc.gpsimd.tensor_tensor(out=rstd[:], in0=var_eps[:], in1=minus_half[:], op=ALU.pow)
+            shift = stats.tile([P, TILES], F32)
+            nc.gpsimd.tensor_tensor(out=shift[:], in0=negmean[:], in1=rstd[:], op=ALU.mult)
             rstd_of[g] = rstd
             shift_of[g] = shift
 
         def normalise(g):
             y = y_pool.tile([P, TILES, FEATURES], F32)
             for j in range(SCALAR_TILES, TILES):
-                nc.vector.tensor_scalar(
+                nc.gpsimd.tensor_scalar(
                     out=y[:, j, :],
                     in0=h_of[g][:, j, :],
                     scalar1=rstd_of[g][:, j : j + 1],
@@ -210,11 +215,11 @@ def tile_fcd_pa_t_kernel(tc, input1, input2, W1_words, W1_scales, b1, out):
 
         with tc.manual_schedule():
             for step in range(-2, N_GROUPS + 2):
-                run(scale_and_shift, step - 1)
                 run(evacuate, step + 1)
                 run(transpose, step + 2)
                 run(add_bias, step)
                 run(quantise_and_multiply, step + 1)
                 run(variance, step)
                 run(normalise, step - 1)
+                run(scale_and_shift, step)
                 run(leaky_relu_and_store, step - 2)

@@ -44,6 +44,7 @@ def tile_fcd_pa_t_kernel(tc, input1, input2, W1_words, W1_scales, b1, out):
         h_pool = ctx.enter_context(tc.tile_pool(name="h", bufs=3))
         y_pool = ctx.enter_context(tc.tile_pool(name="y", bufs=6))
         stats = ctx.enter_context(tc.tile_pool(name="stats", bufs=3))
+        unused = ctx.enter_context(tc.tile_pool(name="unused", bufs=TILES))
         xt_psum = ctx.enter_context(tc.psum_pool(name="xt_psum", bufs=2 * PAIRS))
         h_psum = ctx.enter_context(tc.psum_pool(name="h_psum", bufs=TILES))
 
@@ -51,7 +52,6 @@ def tile_fcd_pa_t_kernel(tc, input1, input2, W1_words, W1_scales, b1, out):
         make_identity(nc, ident[:])
         minus_half = const.tile([P, TILES], F32)
         nc.vector.memset(minus_half[:], -0.5)
-        squares = const.tile([P, FEATURES], F32)
 
         w_words = const.tile([P, 2 * FEATURES], U8, align_bytes=64)
         w_scales = const.tile([P, FEATURES], U8, align_bytes=64)
@@ -145,6 +145,7 @@ def tile_fcd_pa_t_kernel(tc, input1, input2, W1_words, W1_scales, b1, out):
         def variance(g):
             sum_sq = stats.tile([P, TILES], F32)
             for j in range(TILES):
+                squares = unused.tile([P, FEATURES], F32)
                 nc.scalar.activation(
                     out=squares[:],
                     in_=h_of[g][:, j, :],

@@ -24,7 +24,7 @@ SLOPE = 0.2
 
 TILES = 4
 PAIRS = TILES // 2
-SCALAR_TILES = 3
+SCALAR_TILES = 4
 N_GROUPS = ROWS // (TILES * P)
 
 FLOPS = 2 * ROWS * K * FEATURES

@@ -24,7 +24,6 @@ SLOPE = 0.2
 
 TILES = 4
 PAIRS = TILES // 2
-SCALAR_TILES = 4
 N_GROUPS = ROWS // (TILES * P)
 
 FLOPS = 2 * ROWS * K * FEATURES
@@ -50,8 +49,12 @@ def tile_fcd_pa_t_kernel(tc, input1, input2, W1_words, W1_scales, b1, out):
 
         ident = const.tile([P, P], F32)
         make_identity(nc, ident[:])
-        minus_half = const.tile([P, TILES], F32)
-        nc.vector.memset(minus_half[:], -0.5)
+        zero_col = const.tile([P, 1], F32)
+        nc.vector.memset(zero_col[:], 0.0)
+        eps_col = const.tile([P, 1], F32)
+        nc.vector.tensor_scalar(
+            out=eps_col[:], in0=zero_col[:], scalar1=1.0, scalar2=EPS, op0=ALU.mult, op1=ALU.add
+        )
 
         w_words = const.tile([P, 2 * FEATURES], U8, align_bytes=64)
         w_scales = const.tile([P, FEATURES], U8, align_bytes=64)
@@ -126,21 +129,22 @@ def tile_fcd_pa_t_kernel(tc, input1, input2, W1_words, W1_scales, b1, out):
                 )
                 product_of[g].append(product)
 
-        def add_bias(g):
-            h = h_pool.tile([P, TILES, FEATURES], F32)
-            row_sum = stats.tile([P, TILES], F32)
-            for j in range(TILES):
+        def add_bias(g, tiles):
+            if g not in h_of:
+                h = h_pool.tile([P, TILES, FEATURES], F32)
+                row_sum = stats.tile([P, TILES], F32)
+                h_of[g] = h
+                row_sum_of[g] = row_sum
+            for j in tiles:
                 nc.vector.scalar_tensor_tensor(
-                    out=h[:, j, :],
+                    out=h_of[g][:, j, :],
                     in0=product_of[g][j][:],
                     scalar=1.0,
                     in1=bias[:],
                     op0=ALU.mult,
                     op1=ALU.add,
-                    accum_out=row_sum[:, j : j + 1],
+                    accum_out=row_sum_of[g][:, j : j + 1],
                 )
-            h_of[g] = h
-            row_sum_of[g] = row_sum
 
         def variance(g):
             sum_sq = stats.tile([P, TILES], F32)
@@ -156,52 +160,41 @@ def tile_fcd_pa_t_kernel(tc, input1, input2, W1_words, W1_scales, b1, out):
                 )
             sum_sq_of[g] = sum_sq
 
-        def scale_and_shift(g):
-            negmean = stats.tile([P, TILES], F32)
-            nc.gpsimd.tensor_scalar(
-                out=negmean[:],
-                in0=row_sum_of[g][:],
-                scalar1=-1.0 / FEATURES,
-                scalar2=0.0,
-                op0=ALU.mult,
-                op1=ALU.add,
-            )
-            var_eps = stats.tile([P, TILES], F32)
-            nc.gpsimd.tensor_scalar(
-                out=var_eps[:],
-                in0=sum_sq_of[g][:],
-                scalar1=1.0 / FEATURES**3,
-                scalar2=EPS,
-                op0=ALU.mult,
-                op1=ALU.add,
-            )
+        def inverse_deviation(g):
             rstd = stats.tile([P, TILES], F32)
-            nc.gpsimd.tensor_tensor(out=rstd[:], in0=var_eps[:], in1=minus_half[:], op=ALU.pow)
-            shift = stats.tile([P, TILES], F32)
-            nc.gpsimd.tensor_tensor(out=shift[:], in0=negmean[:], in1=rstd[:], op=ALU.mult)
+            nc.scalar.activation(
+                out=rstd[:],
+                in_=sum_sq_of[g][:],
+                func=ACT.Abs_reciprocal_sqrt,
+                bias=eps_col[:],
+                scale=1.0 / FEATURES**3,
+            )
             rstd_of[g] = rstd
-            shift_of[g] = shift
 
-        def normalise(g):
-            y = y_pool.tile([P, TILES, FEATURES], F32)
-            for j in range(SCALAR_TILES, TILES):
-                nc.gpsimd.tensor_scalar(
-                    out=y[:, j, :],
-                    in0=h_of[g][:, j, :],
-                    scalar1=rstd_of[g][:, j : j + 1],
-                    scalar2=shift_of[g][:, j : j + 1],
-                    op0=ALU.mult,
-                    op1=ALU.add,
-                )
-            for j in range(SCALAR_TILES):
+        def shift(g):
+            shifts = stats.tile([P, TILES], F32)
+            nc.vector.scalar_tensor_tensor(
+                out=shifts[:],
+                in0=row_sum_of[g][:],
+                scalar=-1.0 / FEATURES,
+                in1=rstd_of[g][:],
+                op0=ALU.mult,
+                op1=ALU.mult,
+            )
+            shift_of[g] = shifts
+
+        def normalise(g, tiles):
+            if g not in y_of:
+                y = y_pool.tile([P, TILES, FEATURES], F32)
+                y_of[g] = y
+            for j in tiles:
                 nc.scalar.activation(
-                    out=y[:, j, :],
+                    out=y_of[g][:, j, :],
                     in_=h_of[g][:, j, :],
                     func=ACT.Identity,
                     bias=shift_of[g][:, j : j + 1],
                     scale=rstd_of[g][:, j : j + 1],
                 )
-            y_of[g] = y
 
         def leaky_relu_and_store(g):
             flat = y_of[g][:].rearrange("p j f -> p (j f)")
@@ -210,17 +203,20 @@ def tile_fcd_pa_t_kernel(tc, input1, input2, W1_words, W1_scales, b1, out):
             )
             nc.sync.dma_start(out=out_groups[g], in_=y_of[g][:])
 
-        def run(stage, g):
+        def run(stage, g, *tiles):
             if 0 <= g < N_GROUPS:
-                stage(g)
+                stage(g, *tiles)
 
         with tc.manual_schedule():
             for step in range(-2, N_GROUPS + 2):
                 run(evacuate, step + 1)
                 run(transpose, step + 2)
-                run(add_bias, step)
+                run(add_bias, step, (0, 1))
+                run(shift, step - 1)
+                run(add_bias, step, (2, 3))
                 run(quantise_and_multiply, step + 1)
                 run(variance, step)
-                run(normalise, step - 1)
-                run(scale_and_shift, step)
+                run(normalise, step - 1, (0,))
+                run(inverse_deviation, step)
+                run(normalise, step - 1, (1, 2, 3))
                 run(leaky_relu_and_store, step - 2)

@@ -183,6 +183,17 @@ def tile_fcd_pa_t_kernel(tc, input1, input2, W1_words, W1_scales, b1, out):
             )
             shift_of[g] = shifts
 
+        def normalise_on_vector(g, tiles):
+            for j in tiles:
+                nc.vector.tensor_scalar(
+                    out=y_of[g][:, j, :],
+                    in0=h_of[g][:, j, :],
+                    scalar1=rstd_of[g][:, j : j + 1],
+                    scalar2=shift_of[g][:, j : j + 1],
+                    op0=ALU.mult,
+                    op1=ALU.add,
+                )
+
         def normalise(g, tiles):
             if g not in y_of:
                 y = y_pool.tile([P, TILES, FEATURES], F32)
@@ -218,5 +229,6 @@ def tile_fcd_pa_t_kernel(tc, input1, input2, W1_words, W1_scales, b1, out):
                 run(variance, step)
                 run(normalise, step - 1, (0,))
                 run(inverse_deviation, step)
-                run(normalise, step - 1, (1, 2, 3))
+                run(normalise, step - 1, (1, 2))
+                run(normalise_on_vector, step - 1, (3,))
                 run(leaky_relu_and_store, step - 2)

@@ -183,9 +183,9 @@ def tile_fcd_pa_t_kernel(tc, input1, input2, W1_words, W1_scales, b1, out):
             )
             shift_of[g] = shifts
 
-        def normalise_on_vector(g, tiles):
+        def normalise_on_gpsimd(g, tiles):
             for j in tiles:
-                nc.vector.tensor_scalar(
+                nc.gpsimd.tensor_scalar(
                     out=y_of[g][:, j, :],
                     in0=h_of[g][:, j, :],
                     scalar1=rstd_of[g][:, j : j + 1],
@@ -222,13 +222,12 @@ def tile_fcd_pa_t_kernel(tc, input1, input2, W1_words, W1_scales, b1, out):
             for step in range(-2, N_GROUPS + 2):
                 run(evacuate, step + 1)
                 run(transpose, step + 2)
-                run(add_bias, step, (0, 1))
                 run(shift, step - 1)
-                run(add_bias, step, (2, 3))
+                run(add_bias, step, (0, 1, 2, 3))
                 run(quantise_and_multiply, step + 1)
                 run(variance, step)
                 run(normalise, step - 1, (0,))
                 run(inverse_deviation, step)
                 run(normalise, step - 1, (1, 2))
-                run(normalise_on_vector, step - 1, (3,))
+                run(normalise_on_gpsimd, step - 1, (3,))
                 run(leaky_relu_and_store, step - 2)

@@ -207,27 +207,31 @@ def tile_fcd_pa_t_kernel(tc, input1, input2, W1_words, W1_scales, b1, out):
                     scale=rstd_of[g][:, j : j + 1],
                 )
 
-        def leaky_relu_and_store(g):
-            flat = y_of[g][:].rearrange("p j f -> p (j f)")
+        def leaky_relu_and_store(g, first, count):
+            tiles = slice(first, first + count)
+            flat = y_of[g][:, tiles, :].rearrange("p j f -> p (j f)")
             nc.vector.scalar_tensor_tensor(
                 out=flat, in0=flat, scalar=SLOPE, in1=flat, op0=ALU.mult, op1=ALU.max
             )
-            nc.sync.dma_start(out=out_groups[g], in_=y_of[g][:])
+            nc.sync.dma_start(out=out_groups[g][:, tiles, :], in_=y_of[g][:, tiles, :])
 
         def run(stage, g, *tiles):
             if 0 <= g < N_GROUPS:
                 stage(g, *tiles)
 
         with tc.manual_schedule():
-            for step in range(-2, N_GROUPS + 2):
+            for step in range(-2, N_GROUPS + 1):
                 run(evacuate, step + 1)
                 run(transpose, step + 2)
                 run(shift, step - 1)
+                run(normalise, step - 1, (0, 1, 2))
+                run(normalise_on_gpsimd, step - 1, (3,))
                 run(add_bias, step, (0, 1, 2, 3))
                 run(quantise_and_multiply, step + 1)
                 run(variance, step)
-                run(normalise, step - 1, (0,))
                 run(inverse_deviation, step)
-                run(normalise, step - 1, (1, 2))
-                run(normalise_on_gpsimd, step - 1, (3,))
-                run(leaky_relu_and_store, step - 2)
+                if step - 1 < N_GROUPS - 1:
+                    run(leaky_relu_and_store, step - 1, 0, TILES)
+                else:
+                    for j in range(TILES):
+                        run(leaky_relu_and_store, step - 1, j, 1)

@@ -224,8 +224,8 @@ def tile_fcd_pa_t_kernel(tc, input1, input2, W1_words, W1_scales, b1, out):
                 run(evacuate, step + 1)
                 run(transpose, step + 2)
                 run(shift, step - 1)
-                run(normalise, step - 1, (0, 1, 2))
-                run(normalise_on_gpsimd, step - 1, (3,))
+                run(normalise, step - 1, (0, 1))
+                run(normalise_on_gpsimd, step - 1, (2, 3))
                 run(add_bias, step, (0, 1, 2, 3))
                 run(quantise_and_multiply, step + 1)
                 run(variance, step)

@@ -61,12 +61,21 @@ def tile_fcd_pa_t_kernel(tc, input1, input2, W1_words, W1_scales, b1, out):
         nc.vector.memset(w_scales[:].bitcast(I32), 0)
         bias = const.tile([P, FEATURES], BF16)
 
-        x_tiles = []
+        x_pairs = []
         for g in range(N_GROUPS):
-            x_sb = x_pool.tile([P, TILES, K], BF16, name="x%d" % g)
-            nc.sync.dma_start(out=x_sb[:, :, 0:D_IN], in_=x1_groups[g])
-            nc.sync.dma_start(out=x_sb[:, :, D_IN:K], in_=x2_groups[g])
-            x_tiles.append(x_sb)
+            if g == 0:
+                x_pairs.append([])
+                for pair in range(PAIRS):
+                    x_half = x_pool.tile([P, 2, K], BF16, name="x0_%d" % pair)
+                    two = slice(2 * pair, 2 * pair + 2)
+                    nc.sync.dma_start(out=x_half[:, :, 0:D_IN], in_=x1_groups[g][:, two, :])
+                    nc.sync.dma_start(out=x_half[:, :, D_IN:K], in_=x2_groups[g][:, two, :])
+                    x_pairs[g].append(x_half[:])
+            else:
+                x_sb = x_pool.tile([P, TILES, K], BF16, name="x%d" % g)
+                nc.sync.dma_start(out=x_sb[:, :, 0:D_IN], in_=x1_groups[g])
+                nc.sync.dma_start(out=x_sb[:, :, D_IN:K], in_=x2_groups[g])
+                x_pairs.append([x_sb[:, 2 * pair : 2 * pair + 2, :] for pair in range(PAIRS)])
             if g == 0:
                 nc.sync.dma_start(out=w_words[:].bitcast(I32), in_=W1_words[0].bitcast(I32))
                 for quadrant in range(4):
@@ -84,50 +93,54 @@ def tile_fcd_pa_t_kernel(tc, input1, input2, W1_words, W1_scales, b1, out):
         sum_sq_of = {}
         rstd_of = {}
         shift_of = {}
+        negmean_of = {}
         y_of = {}
 
         def transpose(g):
-            x_words = x_tiles[g][:].bitcast(F32)
             xt_banks[g] = []
             for pair in range(PAIRS):
+                x_words = x_pairs[g][pair].bitcast(F32)
                 xt = xt_psum.tile([P, 2, 2, P], F32)
                 for j in range(2):
                     for u in range(2):
-                        nc.tensor.transpose(
-                            xt[:, j, u, :], x_words[:, 2 * pair + j, u:WORDS:2], ident[:]
-                        )
+                        nc.tensor.transpose(xt[:, j, u, :], x_words[:, j, u:WORDS:2], ident[:])
                 xt_banks[g].append(xt)
 
-        def evacuate(g):
-            grouped = quant.tile([P, TILES * K], BF16, align_bytes=64)
-            words = grouped[:].bitcast(F32).rearrange("p (j r u) -> p j r u", j=TILES, u=2)
-            for pair in range(PAIRS):
-                nc.scalar.copy(
-                    out=words[:, 2 * pair : 2 * pair + 2],
-                    in_=xt_banks[g][pair][:].rearrange("p j u r -> p j r u"),
-                )
-            grouped_of[g] = grouped
+        def evacuate(g, pair):
+            if g not in grouped_of:
+                grouped = quant.tile([P, TILES * K], BF16, align_bytes=64)
+                grouped_of[g] = grouped
+            words = grouped_of[g][:].bitcast(F32).rearrange("p (j r u) -> p j r u", j=TILES, u=2)
+            nc.scalar.copy(
+                out=words[:, 2 * pair : 2 * pair + 2],
+                in_=xt_banks[g][pair][:].rearrange("p j u r -> p j r u"),
+            )
 
-        def quantise_and_multiply(g):
+        def quantise_and_multiply(g, calls):
             codes = quant.tile([P, TILES * P], U32, align_bytes=64)
             scales = quant.tile([P, TILES * P], U8, align_bytes=64)
-            nc.vector.quantize_mx(
-                out=codes[:].bitcast(FP8X4), scales=scales[:], in_=grouped_of[g][:]
-            )
             product_of[g] = []
-            for j in range(TILES):
-                rows = slice(j * P, (j + 1) * P)
-                product = h_psum.tile([P, FEATURES], F32)
-                nc.tensor.matmul_mx(
-                    out=product[:],
-                    lhsT=codes[:, rows].bitcast(FP8X4),
-                    lhsT_scale=scales[:, rows],
-                    rhs=w_words[:].bitcast(FP4X4),
-                    rhs_scale=w_scales[:],
-                    start=True,
-                    stop=True,
+            share = TILES // calls
+            for call in range(calls):
+                rows = slice(call * share * P, (call + 1) * share * P)
+                nc.vector.quantize_mx(
+                    out=codes[:, rows].bitcast(FP8X4),
+                    scales=scales[:, rows],
+                    in_=grouped_of[g][:, call * share * K : (call + 1) * share * K],
                 )
-                product_of[g].append(product)
+                for j in range(call * share, (call + 1) * share):
+                    rows = slice(j * P, (j + 1) * P)
+                    product = h_psum.tile([P, FEATURES], F32)
+                    nc.tensor.matmul_mx(
+                        out=product[:],
+                        lhsT=codes[:, rows].bitcast(FP8X4),
+                        lhsT_scale=scales[:, rows],
+                        rhs=w_words[:].bitcast(FP4X4),
+                        rhs_scale=w_scales[:],
+                        start=True,
+                        stop=True,
+                    )
+                    product_of[g].append(product)
 
         def add_bias(g, tiles):
             if g not in h_of:
@@ -171,16 +184,22 @@ def tile_fcd_pa_t_kernel(tc, input1, input2, W1_words, W1_scales, b1, out):
             )
             rstd_of[g] = rstd
 
-        def shift(g):
-            shifts = stats.tile([P, TILES], F32)
-            nc.vector.scalar_tensor_tensor(
-                out=shifts[:],
-                in0=row_sum_of[g][:],
-                scalar=-1.0 / FEATURES,
-                in1=rstd_of[g][:],
-                op0=ALU.mult,
-                op1=ALU.mult,
+        def minus_mean(g):
+            negmean = stats.tile([P, TILES], F32)
+            nc.scalar.activation(
+                out=negmean[:], in_=row_sum_of[g][:], func=ACT.Copy, scale=-1.0 / FEATURES
             )
+            negmean_of[g] = negmean
+
+        def shift(g, tiles):
+            shifts = stats.tile([P, TILES], F32)
+            for j in tiles:
+                nc.scalar.activation(
+                    out=shifts[:, j : j + 1],
+                    in_=rstd_of[g][:, j : j + 1],
+                    func=ACT.Copy,
+                    scale=negmean_of[g][:, j : j + 1],
+                )
             shift_of[g] = shifts
 
         def normalise_on_gpsimd(g, tiles):
@@ -188,10 +207,10 @@ def tile_fcd_pa_t_kernel(tc, input1, input2, W1_words, W1_scales, b1, out):
                 nc.gpsimd.tensor_scalar(
                     out=y_of[g][:, j, :],
                     in0=h_of[g][:, j, :],
-                    scalar1=rstd_of[g][:, j : j + 1],
-                    scalar2=shift_of[g][:, j : j + 1],
-                    op0=ALU.mult,
-                    op1=ALU.add,
+                    scalar1=negmean_of[g][:, j : j + 1],
+                    scalar2=rstd_of[g][:, j : j + 1],
+                    op0=ALU.add,
+                    op1=ALU.mult,
                 )
 
         def normalise(g, tiles):
@@ -220,18 +239,30 @@ def tile_fcd_pa_t_kernel(tc, input1, input2, W1_words, W1_scales, b1, out):
                 stage(g, *tiles)
 
         with tc.manual_schedule():
-            for step in range(-2, N_GROUPS + 1):
-                run(evacuate, step + 1)
+            transpose(0)
+            evacuate(0, 0)
+            evacuate(0, 1)
+            quantise_and_multiply(0, PAIRS)
+            transpose(1)
+            evacuate(1, 0)
+            evacuate(1, 1)
+            for step in range(0, N_GROUPS + 1):
                 run(transpose, step + 2)
-                run(shift, step - 1)
-                run(normalise, step - 1, (0, 1))
-                run(normalise_on_gpsimd, step - 1, (2, 3))
-                run(add_bias, step, (0, 1, 2, 3))
-                run(quantise_and_multiply, step + 1)
-                run(variance, step)
-                run(inverse_deviation, step)
-                if step - 1 < N_GROUPS - 1:
-                    run(leaky_relu_and_store, step - 1, 0, TILES)
+                if step - 1 == N_GROUPS - 1:
+                    run(normalise, step - 1, (0, 1, 2, 3))
                 else:
+                    run(normalise, step - 1, (0, 1))
+                    run(normalise_on_gpsimd, step - 1, (2, 3))
+                run(add_bias, step, (0, 1, 2, 3))
+                run(quantise_and_multiply, step + 1, 1)
+                run(variance, step)
+                run(minus_mean, step)
+                run(evacuate, step + 2, 0)
+                run(inverse_deviation, step)
+                run(shift, step, (0, 1, 2, 3) if step == N_GROUPS - 1 else (0, 1))
+                run(evacuate, step + 2, 1)
+                if step - 1 == N_GROUPS - 1:
                     for j in range(TILES):
                         run(leaky_relu_and_store, step - 1, j, 1)
+                else:
+                    run(leaky_relu_and_store, step - 1, 0, TILES)

@@ -41,7 +41,8 @@ def tile_fcd_pa_t_kernel(tc, input1, input2, W1_words, W1_scales, b1, out):
         x_pool = ctx.enter_context(tc.tile_pool(name="x", bufs=1))
         quant = ctx.enter_context(tc.tile_pool(name="quant", bufs=2))
         h_pool = ctx.enter_context(tc.tile_pool(name="h", bufs=3))
-        y_pool = ctx.enter_context(tc.tile_pool(name="y", bufs=6))
+        y_pool = ctx.enter_context(tc.tile_pool(name="y", bufs=3))
+        out_pool = ctx.enter_context(tc.tile_pool(name="out", bufs=4))
         stats = ctx.enter_context(tc.tile_pool(name="stats", bufs=3))
         unused = ctx.enter_context(tc.tile_pool(name="unused", bufs=TILES))
         xt_psum = ctx.enter_context(tc.psum_pool(name="xt_psum", bufs=2 * PAIRS))
@@ -94,6 +95,7 @@ def tile_fcd_pa_t_kernel(tc, input1, input2, W1_words, W1_scales, b1, out):
         rstd_of = {}
         shift_of = {}
         negmean_of = {}
+        result_of = {}
         y_of = {}
 
         def transpose(g):
@@ -227,12 +229,20 @@ def tile_fcd_pa_t_kernel(tc, input1, input2, W1_words, W1_scales, b1, out):
                 )
 
         def leaky_relu_and_store(g, first, count):
+            if g not in result_of:
+                result = out_pool.tile([P, TILES, FEATURES], F32)
+                result_of[g] = result
             tiles = slice(first, first + count)
             flat = y_of[g][:, tiles, :].rearrange("p j f -> p (j f)")
             nc.vector.scalar_tensor_tensor(
-                out=flat, in0=flat, scalar=SLOPE, in1=flat, op0=ALU.mult, op1=ALU.max
+                out=result_of[g][:, tiles, :].rearrange("p j f -> p (j f)"),
+                in0=flat,
+                scalar=SLOPE,
+                in1=flat,
+                op0=ALU.mult,
+                op1=ALU.max,
             )
-            nc.sync.dma_start(out=out_groups[g][:, tiles, :], in_=y_of[g][:, tiles, :])
+            nc.sync.dma_start(out=out_groups[g][:, tiles, :], in_=result_of[g][:, tiles, :])
 
         def run(stage, g, *tiles):
             if 0 <= g < N_GROUPS:

@@ -61,22 +61,17 @@ def tile_fcd_pa_t_kernel(tc, input1, input2, W1_words, W1_scales, b1, out):
         w_scales = const.tile([P, FEATURES], U8, align_bytes=64)
         nc.vector.memset(w_scales[:].bitcast(I32), 0)
         bias = const.tile([P, FEATURES], BF16)
+        bias_row = const.tile([P, FEATURES], BF16)
+        nc.vector.memset(bias_row[:], 0.0)
+        ones = const.tile([P, P], BF16)
+        nc.vector.memset(ones[:], 1.0)
 
         x_pairs = []
         for g in range(N_GROUPS):
-            if g == 0:
-                x_pairs.append([])
-                for pair in range(PAIRS):
-                    x_half = x_pool.tile([P, 2, K], BF16, name="x0_%d" % pair)
-                    two = slice(2 * pair, 2 * pair + 2)
-                    nc.sync.dma_start(out=x_half[:, :, 0:D_IN], in_=x1_groups[g][:, two, :])
-                    nc.sync.dma_start(out=x_half[:, :, D_IN:K], in_=x2_groups[g][:, two, :])
-                    x_pairs[g].append(x_half[:])
-            else:
-                x_sb = x_pool.tile([P, TILES, K], BF16, name="x%d" % g)
-                nc.sync.dma_start(out=x_sb[:, :, 0:D_IN], in_=x1_groups[g])
-                nc.sync.dma_start(out=x_sb[:, :, D_IN:K], in_=x2_groups[g])
-                x_pairs.append([x_sb[:, 2 * pair : 2 * pair + 2, :] for pair in range(PAIRS)])
+            x_sb = x_pool.tile([P, TILES, K], BF16, name="x%d" % g)
+            nc.sync.dma_start(out=x_sb[:, :, 0:D_IN], in_=x1_groups[g])
+            nc.sync.dma_start(out=x_sb[:, :, D_IN:K], in_=x2_groups[g])
+            x_pairs.append([x_sb[:, 2 * pair : 2 * pair + 2, :] for pair in range(PAIRS)])
             if g == 0:
                 nc.sync.dma_start(out=w_words[:].bitcast(I32), in_=W1_words[0].bitcast(I32))
                 for quadrant in range(4):
@@ -84,7 +79,7 @@ def tile_fcd_pa_t_kernel(tc, input1, input2, W1_words, W1_scales, b1, out):
                         out=w_scales[32 * quadrant : 32 * quadrant + 4, :].bitcast(I32),
                         in_=W1_scales[0, 4 * quadrant : 4 * quadrant + 4, :].bitcast(I32),
                     )
-                nc.sync.dma_start(out=bias[:], in_=b1.partition_broadcast(P))
+                nc.sync.dma_start(out=bias_row[0:1, :], in_=b1.rearrange("(o f) -> o f", o=1))
 
         xt_banks = {}
         grouped_of = {}
@@ -97,6 +92,11 @@ def tile_fcd_pa_t_kernel(tc, input1, input2, W1_words, W1_scales, b1, out):
         negmean_of = {}
         result_of = {}
         y_of = {}
+
+        def spread_bias():
+            product = h_psum.tile([P, FEATURES], F32)
+            nc.tensor.matmul(out=product[:], lhsT=ones[:], rhs=bias_row[:], start=True, stop=True)
+            nc.scalar.copy(out=bias[:], in_=product[:])
 
         def transpose(g):
             xt_banks[g] = []
@@ -252,6 +252,7 @@ def tile_fcd_pa_t_kernel(tc, input1, input2, W1_words, W1_scales, b1, out):
             transpose(0)
             evacuate(0, 0)
             evacuate(0, 1)
+            spread_bias()
             quantise_and_multiply(0, PAIRS)
             transpose(1)
             evacuate(1, 0)

from contextlib import ExitStack

import concourse.mybir as mybir
from concourse.masks import make_identity

F32 = mybir.dt.float32
BF16 = mybir.dt.bfloat16
I32 = mybir.dt.int32
U32 = mybir.dt.uint32
U8 = mybir.dt.uint8
FP8X4 = mybir.dt.float8_e4m3fn_x4
FP4X4 = mybir.dt.float4_e2m1fn_x4
ACT = mybir.ActivationFunctionType
ALU = mybir.AluOpType

P = 128
ROWS = 8192
D_IN = 256
K = 2 * D_IN
WORDS = K // 2
FEATURES = 512
EPS = 1e-5
SLOPE = 0.2

TILES = 4
PAIRS = TILES // 2
N_GROUPS = ROWS // (TILES * P)

FLOPS = 2 * ROWS * K * FEATURES


def tile_fcd_pa_t_kernel(tc, input1, input2, W1_words, W1_scales, b1, out):
    nc = tc.nc

    x1_groups = input1.rearrange("(g p j) o d -> g p j (o d)", p=P, j=TILES)
    x2_groups = input2.rearrange("(g p j) o d -> g p j (o d)", p=P, j=TILES)
    out_groups = out.rearrange("(g p j) o f -> g p j (o f)", p=P, j=TILES)

    with ExitStack() as ctx:
        const = ctx.enter_context(tc.tile_pool(name="const", bufs=1))
        x_pool = ctx.enter_context(tc.tile_pool(name="x", bufs=1))
        quant = ctx.enter_context(tc.tile_pool(name="quant", bufs=2))
        h_pool = ctx.enter_context(tc.tile_pool(name="h", bufs=3))
        y_pool = ctx.enter_context(tc.tile_pool(name="y", bufs=3))
        out_pool = ctx.enter_context(tc.tile_pool(name="out", bufs=4))
        stats = ctx.enter_context(tc.tile_pool(name="stats", bufs=3))
        unused = ctx.enter_context(tc.tile_pool(name="unused", bufs=TILES))
        xt_psum = ctx.enter_context(tc.psum_pool(name="xt_psum", bufs=2 * PAIRS))
        h_psum = ctx.enter_context(tc.psum_pool(name="h_psum", bufs=TILES))

        ident = const.tile([P, P], F32)
        make_identity(nc, ident[:])
        zero_col = const.tile([P, 1], F32)
        nc.vector.memset(zero_col[:], 0.0)
        eps_col = const.tile([P, 1], F32)
        nc.vector.tensor_scalar(
            out=eps_col[:], in0=zero_col[:], scalar1=1.0, scalar2=EPS, op0=ALU.mult, op1=ALU.add
        )

        w_words = const.tile([P, 2 * FEATURES], U8, align_bytes=64)
        w_scales = const.tile([P, FEATURES], U8, align_bytes=64)
        nc.vector.memset(w_scales[:].bitcast(I32), 0)
        bias = const.tile([P, FEATURES], BF16)
        bias_row = const.tile([P, FEATURES], BF16)
        nc.vector.memset(bias_row[:], 0.0)
        ones = const.tile([P, P], BF16)
        nc.vector.memset(ones[:], 1.0)

        x_pairs = []
        for g in range(N_GROUPS):
            x_sb = x_pool.tile([P, TILES, K], BF16, name="x%d" % g)
            nc.sync.dma_start(out=x_sb[:, :, 0:D_IN], in_=x1_groups[g])
            nc.sync.dma_start(out=x_sb[:, :, D_IN:K], in_=x2_groups[g])
            x_pairs.append([x_sb[:, 2 * pair : 2 * pair + 2, :] for pair in range(PAIRS)])
            if g == 0:
                nc.sync.dma_start(out=w_words[:].bitcast(I32), in_=W1_words[0].bitcast(I32))
                for quadrant in range(4):
                    nc.sync.dma_start(
                        out=w_scales[32 * quadrant : 32 * quadrant + 4, :].bitcast(I32),
                        in_=W1_scales[0, 4 * quadrant : 4 * quadrant + 4, :].bitcast(I32),
                    )
                nc.sync.dma_start(out=bias_row[0:1, :], in_=b1.rearrange("(o f) -> o f", o=1))

        xt_banks = {}
        grouped_of = {}
        product_of = {}
        h_of = {}
        row_sum_of = {}
        sum_sq_of = {}
        rstd_of = {}
        shift_of = {}
        negmean_of = {}
        result_of = {}
        y_of = {}

        def spread_bias():
            product = h_psum.tile([P, FEATURES], F32)
            nc.tensor.matmul(out=product[:], lhsT=ones[:], rhs=bias_row[:], start=True, stop=True)
            nc.scalar.copy(out=bias[:], in_=product[:])

        def transpose(g):
            xt_banks[g] = []
            for pair in range(PAIRS):
                x_words = x_pairs[g][pair].bitcast(F32)
                xt = xt_psum.tile([P, 2, 2, P], F32)
                for j in range(2):
                    for u in range(2):
                        nc.tensor.transpose(xt[:, j, u, :], x_words[:, j, u:WORDS:2], ident[:])
                xt_banks[g].append(xt)

        def evacuate(g, pair):
            if g not in grouped_of:
                grouped = quant.tile([P, TILES * K], BF16, align_bytes=64)
                grouped_of[g] = grouped
            words = grouped_of[g][:].bitcast(F32).rearrange("p (j r u) -> p j r u", j=TILES, u=2)
            nc.scalar.copy(
                out=words[:, 2 * pair : 2 * pair + 2],
                in_=xt_banks[g][pair][:].rearrange("p j u r -> p j r u"),
            )

        def quantise_and_multiply(g, calls):
            codes = quant.tile([P, TILES * P], U32, align_bytes=64)
            scales = quant.tile([P, TILES * P], U8, align_bytes=64)
            product_of[g] = []
            share = TILES // calls
            for call in range(calls):
                rows = slice(call * share * P, (call + 1) * share * P)
                nc.vector.quantize_mx(
                    out=codes[:, rows].bitcast(FP8X4),
                    scales=scales[:, rows],
                    in_=grouped_of[g][:, call * share * K : (call + 1) * share * K],
                )
                for j in range(call * share, (call + 1) * share):
                    rows = slice(j * P, (j + 1) * P)
                    product = h_psum.tile([P, FEATURES], F32)
                    nc.tensor.matmul_mx(
                        out=product[:],
                        lhsT=codes[:, rows].bitcast(FP8X4),
                        lhsT_scale=scales[:, rows],
                        rhs=w_words[:].bitcast(FP4X4),
                        rhs_scale=w_scales[:],
                        start=True,
                        stop=True,
                    )
                    product_of[g].append(product)

        def add_bias(g, tiles):
            if g not in h_of:
                h = h_pool.tile([P, TILES, FEATURES], F32)
                row_sum = stats.tile([P, TILES], F32)
                h_of[g] = h
                row_sum_of[g] = row_sum
            for j in tiles:
                nc.vector.scalar_tensor_tensor(
                    out=h_of[g][:, j, :],
                    in0=product_of[g][j][:],
                    scalar=1.0,
                    in1=bias[:],
                    op0=ALU.mult,
                    op1=ALU.add,
                    accum_out=row_sum_of[g][:, j : j + 1],
                )

        def variance(g):
            sum_sq = stats.tile([P, TILES], F32)
            for j in range(TILES):
                squares = unused.tile([P, FEATURES], F32)
                nc.scalar.activation(
                    out=squares[:],
                    in_=h_of[g][:, j, :],
                    func=ACT.Square,
                    bias=row_sum_of[g][:, j : j + 1],
                    scale=-float(FEATURES),
                    accum_out=sum_sq[:, j : j + 1],
                )
            sum_sq_of[g] = sum_sq

        def inverse_deviation(g):
            rstd = stats.tile([P, TILES], F32)
            nc.scalar.activation(
                out=rstd[:],
                in_=sum_sq_of[g][:],
                func=ACT.Abs_reciprocal_sqrt,
                bias=eps_col[:],
                scale=1.0 / FEATURES**3,
            )
            rstd_of[g] = rstd

        def minus_mean(g):
            negmean = stats.tile([P, TILES], F32)
            nc.scalar.activation(
                out=negmean[:], in_=row_sum_of[g][:], func=ACT.Copy, scale=-1.0 / FEATURES
            )
            negmean_of[g] = negmean

        def shift(g, tiles):
            shifts = stats.tile([P, TILES], F32)
            for j in tiles:
                nc.scalar.activation(
                    out=shifts[:, j : j + 1],
                    in_=rstd_of[g][:, j : j + 1],
                    func=ACT.Copy,
                    scale=negmean_of[g][:, j : j + 1],
                )
            shift_of[g] = shifts

        def normalise_on_gpsimd(g, tiles):
            for j in tiles:
                nc.gpsimd.tensor_scalar(
                    out=y_of[g][:, j, :],
                    in0=h_of[g][:, j, :],
                    scalar1=negmean_of[g][:, j : j + 1],
                    scalar2=rstd_of[g][:, j : j + 1],
                    op0=ALU.add,
                    op1=ALU.mult,
                )

        def normalise(g, tiles):
            if g not in y_of:
                y = y_pool.tile([P, TILES, FEATURES], F32)
                y_of[g] = y
            for j in tiles:
                nc.scalar.activation(
                    out=y_of[g][:, j, :],
                    in_=h_of[g][:, j, :],
                    func=ACT.Identity,
                    bias=shift_of[g][:, j : j + 1],
                    scale=rstd_of[g][:, j : j + 1],
                )

        def leaky_relu_and_store(g, first, count):
            if g not in result_of:
                result = out_pool.tile([P, TILES, FEATURES], F32)
                result_of[g] = result
            tiles = slice(first, first + count)
            flat = y_of[g][:, tiles, :].rearrange("p j f -> p (j f)")
            nc.vector.scalar_tensor_tensor(
                out=result_of[g][:, tiles, :].rearrange("p j f -> p (j f)"),
                in0=flat,
                scalar=SLOPE,
                in1=flat,
                op0=ALU.mult,
                op1=ALU.max,
            )
            nc.sync.dma_start(out=out_groups[g][:, tiles, :], in_=result_of[g][:, tiles, :])

        def run(stage, g, *tiles):
            if 0 <= g < N_GROUPS:
                stage(g, *tiles)

        with tc.manual_schedule():
            transpose(0)
            evacuate(0, 0)
            evacuate(0, 1)
            spread_bias()
            quantise_and_multiply(0, PAIRS)
            transpose(1)
            evacuate(1, 0)
            evacuate(1, 1)
            for step in range(0, N_GROUPS + 1):
                run(transpose, step + 2)
                if step - 1 == N_GROUPS - 1:
                    run(normalise, step - 1, (0, 1, 2, 3))
                else:
                    run(normalise, step - 1, (0, 1))
                    run(normalise_on_gpsimd, step - 1, (2, 3))
                run(add_bias, step, (0, 1, 2, 3))
                run(quantise_and_multiply, step + 1, 1)
                run(variance, step)
                run(minus_mean, step)
                run(evacuate, step + 2, 0)
                run(inverse_deviation, step)
                run(shift, step, (0, 1, 2, 3) if step == N_GROUPS - 1 else (0, 1))
                run(evacuate, step + 2, 1)
                if step - 1 == N_GROUPS - 1:
                    for j in range(TILES):
                        run(leaky_relu_and_store, step - 1, j, 1)
                else:
                    run(leaky_relu_and_store, step - 1, 0, TILES)
